import numpy as np
import ml_dtypes


def mxq(x, axis, fmt="e4m3"):
    dtype, down = {"e4m3": (ml_dtypes.float8_e4m3fn, 7), "e5m2": (ml_dtypes.float8_e5m2, 14)}[fmt]
    v = np.moveaxis(np.asarray(x, np.float32).astype(ml_dtypes.bfloat16).astype(np.float64), axis, -1)
    blocks = v.reshape(v.shape[:-1] + (-1, 32))
    amax = np.abs(blocks).max(-1, keepdims=True)
    byte = np.maximum(np.where(amax > 0, np.frexp(amax)[1] - 1 + 127, 0) - down, 1)
    scale = np.exp2(byte - 127.0)
    codes = (blocks / scale).astype(np.float32).astype(dtype).astype(np.float64)
    return np.moveaxis((codes * scale).reshape(v.shape), -1, axis)


WIDE = False


def mx_kscale(k):
    if not WIDE:
        return np.ones(k)
    levels = np.array([10, -10, 5, -5, 0])
    a = np.random.permutation(np.resize(levels, k // 512 * 4)).reshape(k // 512, 4)
    idx = np.arange(k)
    return np.exp2(a[idx // 512, idx % 128 // 32])


BF16 = ml_dtypes.bfloat16


def bf(x):
    return np.asarray(x, np.float32).astype(BF16)


def f64(x):
    return np.asarray(x).astype(np.float64)


B, H, E, V = 512, 1024, 1024, 4096


def sigmoid(v):
    return 1.0 / (1.0 + np.exp(-v))


def draw_w(k, n, div):
    return bf(np.random.standard_normal((k, n)) / np.sqrt(k) / div[:, None])


def setup_inputs():
    s, t = mx_kscale(E), mx_kscale(H)
    one = np.ones(H)
    return {
        "input_data": bf(np.random.standard_normal((B, E)) * s),
        "previous_hidden_state": bf(np.random.standard_normal((B, H)) * t),
        "previous_c_state": bf(np.random.standard_normal((B, H))),
        "w_forget": draw_w(H, H, t),
        "w_input": draw_w(H, H, t),
        "w_c_dash": draw_w(H, H, t),
        "w_forget_c": draw_w(H, H, one),
        "w_input_c": draw_w(H, H, one),
        "w_ip_f": draw_w(E, H, s),
        "w_ip_i": draw_w(E, H, s),
        "w_ip_c_dash": draw_w(E, H, s),
    }


def reference(input_data, previous_hidden_state, previous_c_state, w_forget, w_input, w_c_dash,
              w_forget_c, w_input_c, w_ip_f, w_ip_i, w_ip_c_dash):
    c = f64(previous_c_state)
    xq = mxq(f64(input_data), 1, "e4m3")
    hq = mxq(f64(previous_hidden_state), 1, "e4m3")
    cq = mxq(c, 1, "e4m3")
    zf = (xq @ mxq(f64(w_ip_f), 0, "e4m3")) + (hq @ mxq(f64(w_forget), 0, "e4m3"))
    zi = (xq @ mxq(f64(w_ip_i), 0, "e4m3")) + (hq @ mxq(f64(w_input), 0, "e4m3"))
    zc = (xq @ mxq(f64(w_ip_c_dash), 0, "e4m3")) + (hq @ mxq(f64(w_c_dash), 0, "e4m3"))
    ft = sigmoid(zf + (cq @ mxq(f64(w_forget_c), 0, "e4m3")))
    it = sigmoid(zi + (cq @ mxq(f64(w_input_c), 0, "e4m3")))
    ct_dash = np.tanh(zc)
    return ft * c + it * ct_dash

@@ -1,0 +1,190 @@
+from contextlib import ExitStack
+
+import concourse.mybir as mybir
+from concourse.masks import make_identity
+
+FLOPS = 2 * 512 * 1024 * 1024 * 8
+
+F32 = mybir.dt.float32
+BF16 = mybir.dt.bfloat16
+U32 = mybir.dt.uint32
+U8 = mybir.dt.uint8
+FP8X4 = mybir.dt.float8_e4m3fn_x4
+ACT = mybir.ActivationFunctionType
+
+P = 128
+BT = 4
+K = 1024
+NCOL = 1024
+HALF = 512
+RAW_BUFS = 8
+
+
+def tile_lstm_peephole_build_pa_kernel(
+    tc,
+    input_data,
+    previous_hidden_state,
+    previous_c_state,
+    w_forget,
+    w_input,
+    w_c_dash,
+    w_forget_c,
+    w_input_c,
+    w_ip_f,
+    w_ip_i,
+    w_ip_c_dash,
+    out,
+):
+    nc = tc.nc
+    acts_dram = [input_data, previous_hidden_state, previous_c_state]
+    gates = [
+        ("f", [(0, w_ip_f), (1, w_forget), (2, w_forget_c)]),
+        ("i", [(0, w_ip_i), (1, w_input), (2, w_input_c)]),
+        ("c", [(0, w_ip_c_dash), (1, w_c_dash)]),
+    ]
+    out_v = out.rearrange("(p t) n -> p t n", t=BT)
+
+    with ExitStack() as ctx:
+        keep = ctx.enter_context(tc.tile_pool(name="keep", bufs=1))
+        rawp = ctx.enter_context(tc.tile_pool(name="rawp", bufs=RAW_BUFS))
+        grp = ctx.enter_context(tc.tile_pool(name="grp", bufs=3))
+        cod = ctx.enter_context(tc.tile_pool(name="cod", bufs=6))
+        tmp = ctx.enter_context(tc.tile_pool(name="tmp", bufs=4))
+        psum = ctx.enter_context(tc.psum_pool(name="psum", bufs=1))
+
+        ident = keep.tile([P, P], F32, name="ident")
+        make_identity(nc, ident[:])
+        warm_in = keep.tile([P, 1], F32, name="warm_in")
+        warm_out = keep.tile([P, 1], F32, name="warm_out")
+        nc.vector.memset(warm_in[:], 0.0)
+        nc.scalar.activation(out=warm_out[:], in_=warm_in[:], func=ACT.Sigmoid)
+
+        chunks = []
+        for gi, (gname, pairs) in enumerate(gates):
+            for a, w in pairs:
+                for g in range(2):
+                    chunks.append((gi, a, w, g))
+        act_sb = []
+        raw_tiles = []
+
+        def load_act(a):
+            t = keep.tile([P, BT, K], BF16, name="act%d" % a)
+            nc.sync.dma_start(out=t[:], in_=acts_dram[a].rearrange("(p t) k -> p t k", t=BT))
+            act_sb.append(t)
+
+        def load_chunk(ci):
+            gi, a, w, g = chunks[ci]
+            r = rawp.tile([P, 4, NCOL], BF16, name="raw%d" % ci, tag="raw")
+            nc.sync.dma_start(
+                out=r[:].rearrange("q (u e) n -> q u (e n)", u=2),
+                in_=w[512 * g : 512 * g + 512, :].rearrange("(u q e) n -> q u (e n)", u=2, e=2),
+            )
+            raw_tiles.append(r)
+
+        load_act(0)
+        load_chunk(0)
+        load_act(1)
+        load_chunk(1)
+        load_act(2)
+        for ci in range(2, len(chunks)):
+            load_chunk(ci)
+
+        a_codes = []
+        a_scales = []
+        bank_no = [0]
+        for a in range(3):
+            codes = keep.tile([P, 2, HALF], U32, name="acodes%d" % a, align_bytes=64)
+            scales = keep.tile([P, 2, HALF], U8, name="ascales%d" % a, align_bytes=64)
+            a_codes.append(codes)
+            a_scales.append(scales)
+            words = act_sb[a][:].bitcast(F32)
+            for g in range(2):
+                ga = grp.tile([P, 4 * HALF], BF16, name="ga%d_%d" % (a, g), tag="ga", align_bytes=64)
+                ga_w = ga[:].bitcast(F32).rearrange("q (t m u) -> q t m u", t=BT, u=2)
+                for tp in range(2):
+                    ps = psum.tile(
+                        [P, 2, 2, P], F32, name="tr%d_%d_%d" % (a, g, tp), tag="b%d" % (bank_no[0] % 8)
+                    )
+                    bank_no[0] += 1
+                    for t2 in range(2):
+                        for u in range(2):
+                            lo = 256 * g + 128 * u
+                            nc.tensor.transpose(ps[:, t2, u, :], words[:, 2 * tp + t2, lo : lo + P], ident[:])
+                    dst = ga_w[:, 2 * tp : 2 * tp + 2, :, :]
+                    src = ps[:].rearrange("q t u m -> q t m u")
+                    if tp == 0:
+                        nc.vector.tensor_copy(out=dst, in_=src)
+                    else:
+                        nc.scalar.copy(out=dst, in_=src)
+                nc.vector.quantize_mx(
+                    out=codes[:, g, :].bitcast(FP8X4), scales=scales[:, g, :], in_=ga[:]
+                )
+
+        a_part = keep.tile([P, 8, HALF], F32, name="a_part")
+        i_gate = keep.tile([P, 8, HALF], F32, name="i_gate")
+
+        def unit(ci, nh, acc, first, last):
+            gi, a, w, g = chunks[ci]
+            cols = slice(HALF * nh, HALF * nh + HALF)
+            on_vector = nh == 0
+            gw = grp.tile(
+                [P, HALF, 4], BF16, name="gw%d_%d" % (ci, nh), tag="gv" if on_vector else "gs", align_bytes=64
+            )
+            dst = gw[:].rearrange("p (c i) t -> p c t i", i=4)
+            src = raw_tiles[ci][:, :, cols].rearrange("p t (c i) -> p c t i", i=4)
+            if on_vector:
+                nc.vector.tensor_copy(out=dst, in_=src)
+            else:
+                nc.scalar.copy(out=dst, in_=src)
+            wc = cod.tile([P, HALF], U32, name="wc%d_%d" % (ci, nh), tag="wc", align_bytes=64)
+            ws = cod.tile([P, HALF], U8, name="ws%d_%d" % (ci, nh), tag="ws", align_bytes=64)
+            nc.vector.quantize_mx(
+                out=wc[:].bitcast(FP8X4), scales=ws[:], in_=gw[:].rearrange("p n t -> p (n t)")
+            )
+            for t in range(BT):
+                nc.tensor.matmul_mx(
+                    out=acc[t][:],
+                    lhsT=a_codes[a][:, g, P * t : P * t + P].bitcast(FP8X4),
+                    lhsT_scale=a_scales[a][:, g, P * t : P * t + P],
+                    rhs=wc[:].bitcast(FP8X4),
+                    rhs_scale=ws[:],
+                    start=first,
+                    stop=last,
+                )
+
+        def epilogue(gi, nh, acc):
+            cols = slice(HALF * nh, HALF * nh + HALF)
+            for t in range(BT):
+                b = 4 * nh + t
+                if gi == 0:
+                    nc.scalar.activation(out=a_part[:, b, :], in_=acc[t][:], func=ACT.Sigmoid)
+                    nc.vector.tensor_mul(out=a_part[:, b, :], in0=a_part[:, b, :], in1=act_sb[2][:, t, cols])
+                elif gi == 1:
+                    nc.scalar.activation(out=i_gate[:, b, :], in_=acc[t][:], func=ACT.Sigmoid)
+                else:
+                    cd = tmp.tile([P, HALF], F32, name="cd%d" % b, tag="cd")
+                    nc.scalar.activation(out=cd[:], in_=acc[t][:], func=ACT.Tanh)
+                    nc.vector.tensor_mul(out=cd[:], in0=cd[:], in1=i_gate[:, b, :])
+                    nc.vector.tensor_add(out=a_part[:, b, :], in0=a_part[:, b, :], in1=cd[:])
+                    nc.sync.dma_start(out=out_v[:, t, cols], in_=a_part[:, b, :])
+
+        for gi in range(3):
+            mine = [ci for ci in range(len(chunks)) if chunks[ci][0] == gi]
+            accs = [
+                [
+                    psum.tile([P, HALF], F32, name="acc%d_%d_%d" % (gi, nh, t), tag="b%d" % (4 * nh + t))
+                    for t in range(BT)
+                ]
+                for nh in range(2)
+            ]
+            if gi < 2:
+                for ci in mine:
+                    for nh in range(2):
+                        unit(ci, nh, accs[nh], ci == mine[0], ci == mine[-1])
+                for nh in range(2):
+                    epilogue(gi, nh, accs[nh])
+            else:
+                for nh in range(2):
+                    for ci in mine:
+                        unit(ci, nh, accs[nh], ci == mine[0], ci == mine[-1])
+                    epilogue(gi, nh, accs[nh])

@@ -17,7 +17,15 @@ BT = 4
 K = 1024
 NCOL = 1024
 HALF = 512
+PINNED = True
 RAW_BUFS = 8
+GROUP_BUFS = 4
+CODE_BUFS = 8
+LEAD = 4
+COMBINE_LAG = 3
+TAIL_ON_VECTOR = 2
+ACT_COPY_SPLIT = True
+WEIGHT_FIRST = False
 
 
 def tile_lstm_peephole_build_pa_kernel(
@@ -38,19 +46,21 @@ def tile_lstm_peephole_build_pa_kernel(
     nc = tc.nc
     acts_dram = [input_data, previous_hidden_state, previous_c_state]
     gates = [
-        ("f", [(0, w_ip_f), (1, w_forget), (2, w_forget_c)]),
-        ("i", [(0, w_ip_i), (1, w_input), (2, w_input_c)]),
-        ("c", [(0, w_ip_c_dash), (1, w_c_dash)]),
+        [(0, w_ip_f), (1, w_forget), (2, w_forget_c)],
+        [(0, w_ip_i), (1, w_input), (2, w_input_c)],
+        [(0, w_ip_c_dash), (1, w_c_dash)],
     ]
     out_v = out.rearrange("(p t) n -> p t n", t=BT)
 
     with ExitStack() as ctx:
         keep = ctx.enter_context(tc.tile_pool(name="keep", bufs=1))
         rawp = ctx.enter_context(tc.tile_pool(name="rawp", bufs=RAW_BUFS))
-        grp = ctx.enter_context(tc.tile_pool(name="grp", bufs=3))
-        cod = ctx.enter_context(tc.tile_pool(name="cod", bufs=6))
+        grp = ctx.enter_context(tc.tile_pool(name="grp", bufs=GROUP_BUFS))
+        cod = ctx.enter_context(tc.tile_pool(name="cod", bufs=CODE_BUFS))
         tmp = ctx.enter_context(tc.tile_pool(name="tmp", bufs=4))
         psum = ctx.enter_context(tc.psum_pool(name="psum", bufs=1))
+        if PINNED:
+            ctx.enter_context(tc.manual_schedule())
 
         ident = keep.tile([P, P], F32, name="ident")
         make_identity(nc, ident[:])
@@ -60,10 +70,26 @@ def tile_lstm_peephole_build_pa_kernel(
         nc.scalar.activation(out=warm_out[:], in_=warm_in[:], func=ACT.Sigmoid)
 
         chunks = []
-        for gi, (gname, pairs) in enumerate(gates):
+        for gi, pairs in enumerate(gates):
             for a, w in pairs:
                 for g in range(2):
                     chunks.append((gi, a, w, g))
+
+        items = []
+        for a in range(3):
+            for g in range(2):
+                items.append(("act", a, g))
+        n_units = 0
+        for gi in range(3):
+            mine = [ci for ci in range(len(chunks)) if chunks[ci][0] == gi]
+            if gi < 2:
+                order = [(ci, nh) for ci in mine for nh in range(2)]
+            else:
+                order = [(ci, nh) for nh in range(2) for ci in mine]
+            for ci, nh in order:
+                items.append(("unit", ci, nh, ci == mine[0], ci == mine[-1], n_units))
+                n_units += 1
+
         act_sb = []
         raw_tiles = []
 
@@ -81,66 +107,101 @@ def tile_lstm_peephole_build_pa_kernel(
             )
             raw_tiles.append(r)
 
-        load_act(0)
-        load_chunk(0)
-        load_act(1)
-        load_chunk(1)
-        load_act(2)
-        for ci in range(2, len(chunks)):
+        if WEIGHT_FIRST:
+            load_act(0)
+            load_chunk(0)
+            load_act(1)
+            load_chunk(1)
+            load_act(2)
+            first = 2
+        else:
+            for a in range(3):
+                load_act(a)
+            first = 0
+        for ci in range(first, len(chunks)):
             load_chunk(ci)
 
-        a_codes = []
-        a_scales = []
-        bank_no = [0]
-        for a in range(3):
-            codes = keep.tile([P, 2, HALF], U32, name="acodes%d" % a, align_bytes=64)
-            scales = keep.tile([P, 2, HALF], U8, name="ascales%d" % a, align_bytes=64)
-            a_codes.append(codes)
-            a_scales.append(scales)
-            words = act_sb[a][:].bitcast(F32)
-            for g in range(2):
-                ga = grp.tile([P, 4 * HALF], BF16, name="ga%d_%d" % (a, g), tag="ga", align_bytes=64)
-                ga_w = ga[:].bitcast(F32).rearrange("q (t m u) -> q t m u", t=BT, u=2)
-                for tp in range(2):
-                    ps = psum.tile(
-                        [P, 2, 2, P], F32, name="tr%d_%d_%d" % (a, g, tp), tag="b%d" % (bank_no[0] % 8)
-                    )
-                    bank_no[0] += 1
-                    for t2 in range(2):
-                        for u in range(2):
-                            lo = 256 * g + 128 * u
-                            nc.tensor.transpose(ps[:, t2, u, :], words[:, 2 * tp + t2, lo : lo + P], ident[:])
-                    dst = ga_w[:, 2 * tp : 2 * tp + 2, :, :]
-                    src = ps[:].rearrange("q t u m -> q t m u")
-                    if tp == 0:
-                        nc.vector.tensor_copy(out=dst, in_=src)
-                    else:
-                        nc.scalar.copy(out=dst, in_=src)
-                nc.vector.quantize_mx(
-                    out=codes[:, g, :].bitcast(FP8X4), scales=scales[:, g, :], in_=ga[:]
-                )
-
+        a_codes = [keep.tile([P, 2, HALF], U32, name="acodes%d" % a, align_bytes=64) for a in range(3)]
+        a_scales = [keep.tile([P, 2, HALF], U8, name="ascales%d" % a, align_bytes=64) for a in range(3)]
         a_part = keep.tile([P, 8, HALF], F32, name="a_part")
         i_gate = keep.tile([P, 8, HALF], F32, name="i_gate")
 
-        def unit(ci, nh, acc, first, last):
-            gi, a, w, g = chunks[ci]
-            cols = slice(HALF * nh, HALF * nh + HALF)
-            on_vector = nh == 0
-            gw = grp.tile(
-                [P, HALF, 4], BF16, name="gw%d_%d" % (ci, nh), tag="gv" if on_vector else "gs", align_bytes=64
-            )
-            dst = gw[:].rearrange("p (c i) t -> p c t i", i=4)
-            src = raw_tiles[ci][:, :, cols].rearrange("p t (c i) -> p c t i", i=4)
-            if on_vector:
-                nc.vector.tensor_copy(out=dst, in_=src)
+        state = {}
+        accs = {}
+        n_banks = [0]
+
+        def transposes(i):
+            kind, a, g = items[i]
+            words = act_sb[a][:].bitcast(F32)
+            banks = []
+            for tp in range(2):
+                ps = psum.tile([P, 2, 2, P], F32, name="tr%d_%d_%d" % (a, g, tp), tag="b%d" % (n_banks[0] % 8))
+                n_banks[0] += 1
+                for t2 in range(2):
+                    for u in range(2):
+                        lo = 256 * g + 128 * u
+                        nc.tensor.transpose(ps[:, t2, u, :], words[:, 2 * tp + t2, lo : lo + P], ident[:])
+                banks.append(ps)
+            state[("tr", i)] = banks
+
+        def group(i):
+            it = items[i]
+            if it[0] == "act":
+                kind, a, g = it
+                ga = grp.tile([P, 4 * HALF], BF16, name="ga%d_%d" % (a, g), tag="ga", align_bytes=64)
+                ga_w = ga[:].bitcast(F32).rearrange("q (t m u) -> q t m u", t=BT, u=2)
+                for tp in range(2):
+                    dst = ga_w[:, 2 * tp : 2 * tp + 2, :, :]
+                    src = state[("tr", i)][tp][:].rearrange("q t u m -> q t m u")
+                    if ACT_COPY_SPLIT and tp == 0:
+                        nc.vector.tensor_copy(out=dst, in_=src)
+                    else:
+                        nc.scalar.copy(out=dst, in_=src)
+                state[("g", i)] = ga
             else:
-                nc.scalar.copy(out=dst, in_=src)
-            wc = cod.tile([P, HALF], U32, name="wc%d_%d" % (ci, nh), tag="wc", align_bytes=64)
-            ws = cod.tile([P, HALF], U8, name="ws%d_%d" % (ci, nh), tag="ws", align_bytes=64)
-            nc.vector.quantize_mx(
-                out=wc[:].bitcast(FP8X4), scales=ws[:], in_=gw[:].rearrange("p n t -> p (n t)")
-            )
+                kind, ci, nh, is_first, is_last, un = it
+                cols = slice(HALF * nh, HALF * nh + HALF)
+                on_vector = un % 2 == 0 or un >= n_units - TAIL_ON_VECTOR
+                gw = grp.tile(
+                    [P, HALF, 4], BF16, name="gw%d" % un, tag="gv" if on_vector else "gs", align_bytes=64
+                )
+                dst = gw[:].rearrange("p (c i) t -> p c t i", i=4)
+                src = raw_tiles[ci][:, :, cols].rearrange("p t (c i) -> p c t i", i=4)
+                if on_vector:
+                    nc.vector.tensor_copy(out=dst, in_=src)
+                else:
+                    nc.scalar.copy(out=dst, in_=src)
+                state[("g", i)] = gw
+
+        def quantise(i):
+            it = items[i]
+            if it[0] == "act":
+                kind, a, g = it
+                nc.vector.quantize_mx(
+                    out=a_codes[a][:, g, :].bitcast(FP8X4), scales=a_scales[a][:, g, :], in_=state[("g", i)][:]
+                )
+            else:
+                un = it[5]
+                wc = cod.tile([P, HALF], U32, name="wc%d" % un, tag="wc", align_bytes=64)
+                ws = cod.tile([P, HALF], U8, name="ws%d" % un, tag="ws", align_bytes=64)
+                nc.vector.quantize_mx(
+                    out=wc[:].bitcast(FP8X4), scales=ws[:], in_=state[("g", i)][:].rearrange("p n t -> p (n t)")
+                )
+                state[("q", i)] = (wc, ws)
+
+        def multiply(i):
+            it = items[i]
+            if it[0] == "act":
+                return
+            kind, ci, nh, is_first, is_last, un = it
+            gi, a, w, g = chunks[ci]
+            if is_first:
+                accs[(gi, nh)] = [
+                    psum.tile([P, HALF], F32, name="acc%d_%d_%d" % (gi, nh, t), tag="b%d" % (4 * nh + t))
+                    for t in range(BT)
+                ]
+            acc = accs[(gi, nh)]
+            wc, ws = state[("q", i)]
             for t in range(BT):
                 nc.tensor.matmul_mx(
                     out=acc[t][:],
@@ -148,43 +209,47 @@ def tile_lstm_peephole_build_pa_kernel(
                     lhsT_scale=a_scales[a][:, g, P * t : P * t + P],
                     rhs=wc[:].bitcast(FP8X4),
                     rhs_scale=ws[:],
-                    start=first,
-                    stop=last,
+                    start=is_first,
+                    stop=is_last,
                 )
+            if is_last:
+                for t in range(BT):
+                    b = 4 * nh + t
+                    if gi == 0:
+                        nc.scalar.activation(out=a_part[:, b, :], in_=acc[t][:], func=ACT.Sigmoid)
+                    elif gi == 1:
+                        nc.scalar.activation(out=i_gate[:, b, :], in_=acc[t][:], func=ACT.Sigmoid)
+                    else:
+                        cd = tmp.tile([P, HALF], F32, name="cd%d" % b, tag="cd")
+                        nc.scalar.activation(out=cd[:], in_=acc[t][:], func=ACT.Tanh)
+                        state[("cd", b)] = cd
 
-        def epilogue(gi, nh, acc):
+        def combine(i):
+            it = items[i]
+            if it[0] == "act" or not it[4]:
+                return
+            kind, ci, nh, is_first, is_last, un = it
+            gi = chunks[ci][0]
             cols = slice(HALF * nh, HALF * nh + HALF)
             for t in range(BT):
                 b = 4 * nh + t
                 if gi == 0:
-                    nc.scalar.activation(out=a_part[:, b, :], in_=acc[t][:], func=ACT.Sigmoid)
                     nc.vector.tensor_mul(out=a_part[:, b, :], in0=a_part[:, b, :], in1=act_sb[2][:, t, cols])
-                elif gi == 1:
-                    nc.scalar.activation(out=i_gate[:, b, :], in_=acc[t][:], func=ACT.Sigmoid)
-                else:
-                    cd = tmp.tile([P, HALF], F32, name="cd%d" % b, tag="cd")
-                    nc.scalar.activation(out=cd[:], in_=acc[t][:], func=ACT.Tanh)
+                elif gi == 2:
+                    cd = state[("cd", b)]
                     nc.vector.tensor_mul(out=cd[:], in0=cd[:], in1=i_gate[:, b, :])
                     nc.vector.tensor_add(out=a_part[:, b, :], in0=a_part[:, b, :], in1=cd[:])
                     nc.sync.dma_start(out=out_v[:, t, cols], in_=a_part[:, b, :])
 
-        for gi in range(3):
-            mine = [ci for ci in range(len(chunks)) if chunks[ci][0] == gi]
-            accs = [
-                [
-                    psum.tile([P, HALF], F32, name="acc%d_%d_%d" % (gi, nh, t), tag="b%d" % (4 * nh + t))
-                    for t in range(BT)
-                ]
-                for nh in range(2)
-            ]
-            if gi < 2:
-                for ci in mine:
-                    for nh in range(2):
-                        unit(ci, nh, accs[nh], ci == mine[0], ci == mine[-1])
-                for nh in range(2):
-                    epilogue(gi, nh, accs[nh])
-            else:
-                for nh in range(2):
-                    for ci in mine:
-                        unit(ci, nh, accs[nh], ci == mine[0], ci == mine[-1])
-                    epilogue(gi, nh, accs[nh])
+        n = len(items)
+        for s in range(-LEAD - 1, n + COMBINE_LAG + 1):
+            if 0 <= s + LEAD + 1 < n and items[s + LEAD + 1][0] == "act":
+                transposes(s + LEAD + 1)
+            if 0 <= s < n:
+                quantise(s)
+            if 0 <= s + LEAD < n:
+                group(s + LEAD)
+            if 0 <= s - 1 < n:
+                multiply(s - 1)
+            if 0 <= s - 1 - COMBINE_LAG < n:
+                combine(s - 1 - COMBINE_LAG)

@@ -13,19 +13,17 @@ FP8X4 = mybir.dt.float8_e4m3fn_x4
 ACT = mybir.ActivationFunctionType
 
 P = 128
+PACK = 4
 BT = 4
 K = 1024
+K_PASS = 512
 NCOL = 1024
 HALF = 512
 PINNED = True
 RAW_BUFS = 8
-GROUP_BUFS = 4
-CODE_BUFS = 8
-LEAD = 4
-COMBINE_LAG = 3
-TAIL_ON_VECTOR = 2
-ACT_COPY_SPLIT = True
-WEIGHT_FIRST = False
+LEAD = 2
+COMBINE_LAG = 1
+CODE_BUFS = 4
 
 
 def tile_lstm_peephole_build_pa_kernel(
@@ -55,7 +53,7 @@ def tile_lstm_peephole_build_pa_kernel(
     with ExitStack() as ctx:
         keep = ctx.enter_context(tc.tile_pool(name="keep", bufs=1))
         rawp = ctx.enter_context(tc.tile_pool(name="rawp", bufs=RAW_BUFS))
-        grp = ctx.enter_context(tc.tile_pool(name="grp", bufs=GROUP_BUFS))
+        grp = ctx.enter_context(tc.tile_pool(name="grp", bufs=LEAD + 1))
         cod = ctx.enter_context(tc.tile_pool(name="cod", bufs=CODE_BUFS))
         tmp = ctx.enter_context(tc.tile_pool(name="tmp", bufs=4))
         psum = ctx.enter_context(tc.psum_pool(name="psum", bufs=1))
@@ -70,186 +68,154 @@ def tile_lstm_peephole_build_pa_kernel(
         nc.scalar.activation(out=warm_out[:], in_=warm_in[:], func=ACT.Sigmoid)
 
         chunks = []
-        for gi, pairs in enumerate(gates):
-            for a, w in pairs:
+        for gi, products in enumerate(gates):
+            for a, w in products:
                 for g in range(2):
                     chunks.append((gi, a, w, g))
 
-        items = []
-        for a in range(3):
-            for g in range(2):
-                items.append(("act", a, g))
-        n_units = 0
+        pairs = []
         for gi in range(3):
             mine = [ci for ci in range(len(chunks)) if chunks[ci][0] == gi]
             if gi < 2:
-                order = [(ci, nh) for ci in mine for nh in range(2)]
+                for ci in mine:
+                    pairs.append([(ci, nh, ci == mine[0], ci == mine[-1]) for nh in range(2)])
             else:
-                order = [(ci, nh) for nh in range(2) for ci in mine]
-            for ci, nh in order:
-                items.append(("unit", ci, nh, ci == mine[0], ci == mine[-1], n_units))
-                n_units += 1
+                for nh in range(2):
+                    for j in range(0, len(mine), 2):
+                        pairs.append([(ci, nh, ci == mine[0], ci == mine[-1]) for ci in mine[j : j + 2]])
+        n_pairs = len(pairs)
 
         act_sb = []
-        raw_tiles = []
-
-        def load_act(a):
+        for a in range(3):
             t = keep.tile([P, BT, K], BF16, name="act%d" % a)
             nc.sync.dma_start(out=t[:], in_=acts_dram[a].rearrange("(p t) k -> p t k", t=BT))
             act_sb.append(t)
-
-        def load_chunk(ci):
-            gi, a, w, g = chunks[ci]
-            r = rawp.tile([P, 4, NCOL], BF16, name="raw%d" % ci, tag="raw")
+        raw_tiles = []
+        for ci, (gi, a, w, g) in enumerate(chunks):
+            r = rawp.tile([P, PACK, NCOL], BF16, name="raw%d" % ci, tag="raw")
             nc.sync.dma_start(
                 out=r[:].rearrange("q (u e) n -> q u (e n)", u=2),
-                in_=w[512 * g : 512 * g + 512, :].rearrange("(u q e) n -> q u (e n)", u=2, e=2),
+                in_=w[K_PASS * g : K_PASS * (g + 1), :].rearrange("(u q e) n -> q u (e n)", u=2, e=2),
             )
             raw_tiles.append(r)
 
-        if WEIGHT_FIRST:
-            load_act(0)
-            load_chunk(0)
-            load_act(1)
-            load_chunk(1)
-            load_act(2)
-            first = 2
-        else:
-            for a in range(3):
-                load_act(a)
-            first = 0
-        for ci in range(first, len(chunks)):
-            load_chunk(ci)
-
-        a_codes = [keep.tile([P, 2, HALF], U32, name="acodes%d" % a, align_bytes=64) for a in range(3)]
-        a_scales = [keep.tile([P, 2, HALF], U8, name="ascales%d" % a, align_bytes=64) for a in range(3)]
-        a_part = keep.tile([P, 8, HALF], F32, name="a_part")
-        i_gate = keep.tile([P, 8, HALF], F32, name="i_gate")
-
-        state = {}
-        accs = {}
-        n_banks = [0]
-
-        def transposes(i):
-            kind, a, g = items[i]
+        a_codes = []
+        a_scales = []
+        n_banks = 0
+        for a in range(3):
+            codes = keep.tile([P, 2, HALF], U32, name="acodes%d" % a, align_bytes=64)
+            scales = keep.tile([P, 2, HALF], U8, name="ascales%d" % a, align_bytes=64)
+            a_codes.append(codes)
+            a_scales.append(scales)
             words = act_sb[a][:].bitcast(F32)
-            banks = []
-            for tp in range(2):
-                ps = psum.tile([P, 2, 2, P], F32, name="tr%d_%d_%d" % (a, g, tp), tag="b%d" % (n_banks[0] % 8))
-                n_banks[0] += 1
-                for t2 in range(2):
-                    for u in range(2):
-                        lo = 256 * g + 128 * u
-                        nc.tensor.transpose(ps[:, t2, u, :], words[:, 2 * tp + t2, lo : lo + P], ident[:])
-                banks.append(ps)
-            state[("tr", i)] = banks
-
-        def group(i):
-            it = items[i]
-            if it[0] == "act":
-                kind, a, g = it
-                ga = grp.tile([P, 4 * HALF], BF16, name="ga%d_%d" % (a, g), tag="ga", align_bytes=64)
+            grouped = []
+            for g in range(2):
+                ga = keep.tile([P, PACK * HALF], BF16, name="ga%d_%d" % (a, g), tag="ga%d" % g, align_bytes=64)
                 ga_w = ga[:].bitcast(F32).rearrange("q (t m u) -> q t m u", t=BT, u=2)
                 for tp in range(2):
+                    ps = psum.tile([P, 2, 2, P], F32, name="tr%d_%d_%d" % (a, g, tp), tag="b%d" % (n_banks % 8))
+                    n_banks += 1
+                    for t2 in range(2):
+                        for u in range(2):
+                            lo = 256 * g + P * u
+                            nc.tensor.transpose(ps[:, t2, u, :], words[:, 2 * tp + t2, lo : lo + P], ident[:])
                     dst = ga_w[:, 2 * tp : 2 * tp + 2, :, :]
-                    src = state[("tr", i)][tp][:].rearrange("q t u m -> q t m u")
-                    if ACT_COPY_SPLIT and tp == 0:
+                    src = ps[:].rearrange("q t u m -> q t m u")
+                    if tp == 0:
                         nc.vector.tensor_copy(out=dst, in_=src)
                     else:
                         nc.scalar.copy(out=dst, in_=src)
-                state[("g", i)] = ga
-            else:
-                kind, ci, nh, is_first, is_last, un = it
-                cols = slice(HALF * nh, HALF * nh + HALF)
-                on_vector = un % 2 == 0 or un >= n_units - TAIL_ON_VECTOR
-                gw = grp.tile(
-                    [P, HALF, 4], BF16, name="gw%d" % un, tag="gv" if on_vector else "gs", align_bytes=64
+                grouped.append(ga)
+            for g in range(2):
+                nc.vector.quantize_mx(
+                    out=codes[:, g, :].bitcast(FP8X4), scales=scales[:, g, :], in_=grouped[g][:]
                 )
-                dst = gw[:].rearrange("p (c i) t -> p c t i", i=4)
-                src = raw_tiles[ci][:, :, cols].rearrange("p t (c i) -> p c t i", i=4)
-                if on_vector:
+
+        a_part = keep.tile([P, 8, HALF], F32, name="a_part")
+        i_gate = keep.tile([P, 8, HALF], F32, name="i_gate")
+        grouped_w = {}
+        coded_w = {}
+        accs = {}
+        c_dash = {}
+
+        def regroup(s):
+            gw = grp.tile([P, 2, HALF, PACK], BF16, name="gw%d" % s, tag="gw", align_bytes=64)
+            for j, (ci, nh, opens, closes) in enumerate(pairs[s]):
+                dst = gw[:, j, :, :].rearrange("p (c i) t -> p c t i", i=4)
+                src = raw_tiles[ci][:, :, HALF * nh : HALF * (nh + 1)].rearrange("p t (c i) -> p c t i", i=4)
+                if j == 0 or s == n_pairs - 1:
                     nc.vector.tensor_copy(out=dst, in_=src)
                 else:
                     nc.scalar.copy(out=dst, in_=src)
-                state[("g", i)] = gw
+            grouped_w[s] = gw
 
-        def quantise(i):
-            it = items[i]
-            if it[0] == "act":
-                kind, a, g = it
-                nc.vector.quantize_mx(
-                    out=a_codes[a][:, g, :].bitcast(FP8X4), scales=a_scales[a][:, g, :], in_=state[("g", i)][:]
-                )
-            else:
-                un = it[5]
-                wc = cod.tile([P, HALF], U32, name="wc%d" % un, tag="wc", align_bytes=64)
-                ws = cod.tile([P, HALF], U8, name="ws%d" % un, tag="ws", align_bytes=64)
-                nc.vector.quantize_mx(
-                    out=wc[:].bitcast(FP8X4), scales=ws[:], in_=state[("g", i)][:].rearrange("p n t -> p (n t)")
-                )
-                state[("q", i)] = (wc, ws)
+        def quantise(s):
+            wc = cod.tile([P, 2, HALF], U32, name="wc%d" % s, tag="wc", align_bytes=64)
+            ws = cod.tile([P, 2, HALF], U8, name="ws%d" % s, tag="ws", align_bytes=64)
+            nc.vector.quantize_mx(
+                out=wc[:].rearrange("p j n -> p (j n)").bitcast(FP8X4),
+                scales=ws[:].rearrange("p j n -> p (j n)"),
+                in_=grouped_w[s][:].rearrange("p j n t -> p (j n t)"),
+            )
+            coded_w[s] = (wc, ws)
 
-        def multiply(i):
-            it = items[i]
-            if it[0] == "act":
-                return
-            kind, ci, nh, is_first, is_last, un = it
-            gi, a, w, g = chunks[ci]
-            if is_first:
-                accs[(gi, nh)] = [
-                    psum.tile([P, HALF], F32, name="acc%d_%d_%d" % (gi, nh, t), tag="b%d" % (4 * nh + t))
-                    for t in range(BT)
-                ]
-            acc = accs[(gi, nh)]
-            wc, ws = state[("q", i)]
-            for t in range(BT):
-                nc.tensor.matmul_mx(
-                    out=acc[t][:],
-                    lhsT=a_codes[a][:, g, P * t : P * t + P].bitcast(FP8X4),
-                    lhsT_scale=a_scales[a][:, g, P * t : P * t + P],
-                    rhs=wc[:].bitcast(FP8X4),
-                    rhs_scale=ws[:],
-                    start=is_first,
-                    stop=is_last,
-                )
-            if is_last:
+        def multiply(s):
+            wc, ws = coded_w[s]
+            for j, (ci, nh, opens, closes) in enumerate(pairs[s]):
+                gi, a, w, g = chunks[ci]
+                if opens:
+                    accs[(gi, nh)] = [
+                        psum.tile([P, HALF], F32, name="acc%d_%d_%d" % (gi, nh, t), tag="b%d" % (BT * nh + t))
+                        for t in range(BT)
+                    ]
                 for t in range(BT):
-                    b = 4 * nh + t
+                    nc.tensor.matmul_mx(
+                        out=accs[(gi, nh)][t][:],
+                        lhsT=a_codes[a][:, g, P * t : P * (t + 1)].bitcast(FP8X4),
+                        lhsT_scale=a_scales[a][:, g, P * t : P * (t + 1)],
+                        rhs=wc[:, j, :].bitcast(FP8X4),
+                        rhs_scale=ws[:, j, :],
+                        start=opens,
+                        stop=closes,
+                    )
+            for ci, nh, opens, closes in pairs[s]:
+                gi = chunks[ci][0]
+                if closes:
+                    for t in range(BT):
+                        b = BT * nh + t
+                        acc = accs[(gi, nh)][t]
+                        if gi == 0:
+                            nc.scalar.activation(out=a_part[:, b, :], in_=acc[:], func=ACT.Sigmoid)
+                        elif gi == 1:
+                            nc.scalar.activation(out=i_gate[:, b, :], in_=acc[:], func=ACT.Sigmoid)
+                        else:
+                            if t % 2 == 0:
+                                c_dash[b] = tmp.tile([P, 2, HALF], F32, name="cd%d" % b, tag="cd")
+                            nc.scalar.activation(out=c_dash[b - t % 2][:, t % 2, :], in_=acc[:], func=ACT.Tanh)
+
+        def combine(s):
+            for ci, nh, opens, closes in pairs[s]:
+                gi = chunks[ci][0]
+                if not closes or gi == 1:
+                    continue
+                cols = slice(HALF * nh, HALF * (nh + 1))
+                for t in range(0, BT, 2):
+                    b = BT * nh + t
+                    part = a_part[:, b : b + 2, :]
                     if gi == 0:
-                        nc.scalar.activation(out=a_part[:, b, :], in_=acc[t][:], func=ACT.Sigmoid)
-                    elif gi == 1:
-                        nc.scalar.activation(out=i_gate[:, b, :], in_=acc[t][:], func=ACT.Sigmoid)
+                        nc.vector.tensor_mul(out=part, in0=part, in1=act_sb[2][:, t : t + 2, cols])
                     else:
-                        cd = tmp.tile([P, HALF], F32, name="cd%d" % b, tag="cd")
-                        nc.scalar.activation(out=cd[:], in_=acc[t][:], func=ACT.Tanh)
-                        state[("cd", b)] = cd
+                        cd = c_dash[b]
+                        nc.vector.tensor_mul(out=cd[:], in0=cd[:], in1=i_gate[:, b : b + 2, :])
+                        nc.vector.tensor_add(out=part, in0=part, in1=cd[:])
+                        nc.sync.dma_start(out=out_v[:, t : t + 2, cols], in_=part)
 
-        def combine(i):
-            it = items[i]
-            if it[0] == "act" or not it[4]:
-                return
-            kind, ci, nh, is_first, is_last, un = it
-            gi = chunks[ci][0]
-            cols = slice(HALF * nh, HALF * nh + HALF)
-            for t in range(BT):
-                b = 4 * nh + t
-                if gi == 0:
-                    nc.vector.tensor_mul(out=a_part[:, b, :], in0=a_part[:, b, :], in1=act_sb[2][:, t, cols])
-                elif gi == 2:
-                    cd = state[("cd", b)]
-                    nc.vector.tensor_mul(out=cd[:], in0=cd[:], in1=i_gate[:, b, :])
-                    nc.vector.tensor_add(out=a_part[:, b, :], in0=a_part[:, b, :], in1=cd[:])
-                    nc.sync.dma_start(out=out_v[:, t, cols], in_=a_part[:, b, :])
-
-        n = len(items)
-        for s in range(-LEAD - 1, n + COMBINE_LAG + 1):
-            if 0 <= s + LEAD + 1 < n and items[s + LEAD + 1][0] == "act":
-                transposes(s + LEAD + 1)
-            if 0 <= s < n:
+        for s in range(-LEAD, n_pairs + COMBINE_LAG + 1):
+            if 0 <= s < n_pairs:
                 quantise(s)
-            if 0 <= s + LEAD < n:
-                group(s + LEAD)
-            if 0 <= s - 1 < n:
+            if 0 <= s + LEAD < n_pairs:
+                regroup(s + LEAD)
+            if 0 <= s - 1 < n_pairs:
                 multiply(s - 1)
-            if 0 <= s - 1 - COMBINE_LAG < n:
+            if 0 <= s - 1 - COMBINE_LAG < n_pairs:
                 combine(s - 1 - COMBINE_LAG)

@@ -94,8 +94,8 @@ def tile_lstm_peephole_build_pa_kernel(
         for ci, (gi, a, w, g) in enumerate(chunks):
             r = rawp.tile([P, PACK, NCOL], BF16, name="raw%d" % ci, tag="raw")
             nc.sync.dma_start(
-                out=r[:].rearrange("q (u e) n -> q u (e n)", u=2),
-                in_=w[K_PASS * g : K_PASS * (g + 1), :].rearrange("(u q e) n -> q u (e n)", u=2, e=2),
+                out=r[:].rearrange("q j n -> q (j n)"),
+                in_=w[K_PASS * g : K_PASS * (g + 1), :].rearrange("(q j) n -> q (j n)", j=PACK),
             )
             raw_tiles.append(r)
 
@@ -107,7 +107,7 @@ def tile_lstm_peephole_build_pa_kernel(
             scales = keep.tile([P, 2, HALF], U8, name="ascales%d" % a, align_bytes=64)
             a_codes.append(codes)
             a_scales.append(scales)
-            words = act_sb[a][:].bitcast(F32)
+            words = act_sb[a][:].bitcast(F32).rearrange("p t (g q u) -> p t g u q", g=2, u=2)
             grouped = []
             for g in range(2):
                 ga = keep.tile([P, PACK * HALF], BF16, name="ga%d_%d" % (a, g), tag="ga%d" % g, align_bytes=64)
@@ -117,8 +117,7 @@ def tile_lstm_peephole_build_pa_kernel(
                     n_banks += 1
                     for t2 in range(2):
                         for u in range(2):
-                            lo = 256 * g + P * u
-                            nc.tensor.transpose(ps[:, t2, u, :], words[:, 2 * tp + t2, lo : lo + P], ident[:])
+                            nc.tensor.transpose(ps[:, t2, u, :], words[:, 2 * tp + t2, g, u, :], ident[:])
                     dst = ga_w[:, 2 * tp : 2 * tp + 2, :, :]
                     src = ps[:].rearrange("q t u m -> q t m u")
                     if tp == 0:

@@ -140,8 +140,8 @@ def tile_lstm_peephole_build_pa_kernel(
         def regroup(s):
             gw = grp.tile([P, 2, HALF, PACK], BF16, name="gw%d" % s, tag="gw", align_bytes=64)
             for j, (ci, nh, opens, closes) in enumerate(pairs[s]):
-                dst = gw[:, j, :, :].rearrange("p (c i) t -> p c t i", i=4)
-                src = raw_tiles[ci][:, :, HALF * nh : HALF * (nh + 1)].rearrange("p t (c i) -> p c t i", i=4)
+                dst = gw[:, j, :, :].rearrange("p (c i) t -> p c t i", i=8)
+                src = raw_tiles[ci][:, :, HALF * nh : HALF * (nh + 1)].rearrange("p t (c i) -> p c t i", i=8)
                 if j == 0 or s == n_pairs - 1:
                     nc.vector.tensor_copy(out=dst, in_=src)
                 else:

@@ -19,11 +19,16 @@ K = 1024
 K_PASS = 512
 NCOL = 1024
 HALF = 512
-PINNED = True
+QUARTER = 256
 RAW_BUFS = 8
 LEAD = 2
-COMBINE_LAG = 1
-CODE_BUFS = 4
+V_FIRST = 768
+V_MID = 512
+V_LAST = 1024
+V_C = 512
+GRP_BUFS = 3
+CODE_BUFS = 6
+RUN = 8
 
 
 def tile_lstm_peephole_build_pa_kernel(
@@ -53,12 +58,12 @@ def tile_lstm_peephole_build_pa_kernel(
     with ExitStack() as ctx:
         keep = ctx.enter_context(tc.tile_pool(name="keep", bufs=1))
         rawp = ctx.enter_context(tc.tile_pool(name="rawp", bufs=RAW_BUFS))
-        grp = ctx.enter_context(tc.tile_pool(name="grp", bufs=LEAD + 1))
+        grp = ctx.enter_context(tc.tile_pool(name="grp", bufs=GRP_BUFS))
+        agrp = ctx.enter_context(tc.tile_pool(name="agrp", bufs=2))
         cod = ctx.enter_context(tc.tile_pool(name="cod", bufs=CODE_BUFS))
         tmp = ctx.enter_context(tc.tile_pool(name="tmp", bufs=4))
         psum = ctx.enter_context(tc.psum_pool(name="psum", bufs=1))
-        if PINNED:
-            ctx.enter_context(tc.manual_schedule())
+        ctx.enter_context(tc.manual_schedule())
 
         ident = keep.tile([P, P], F32, name="ident")
         make_identity(nc, ident[:])
@@ -73,148 +78,218 @@ def tile_lstm_peephole_build_pa_kernel(
                 for g in range(2):
                     chunks.append((gi, a, w, g))
 
-        pairs = []
+        jobs = []
         for gi in range(3):
             mine = [ci for ci in range(len(chunks)) if chunks[ci][0] == gi]
             if gi < 2:
                 for ci in mine:
-                    pairs.append([(ci, nh, ci == mine[0], ci == mine[-1]) for nh in range(2)])
+                    jobs.append([(ci, HALF * nh, HALF, ci == mine[0], ci == mine[-1]) for nh in range(2)])
             else:
-                for nh in range(2):
-                    for j in range(0, len(mine), 2):
-                        pairs.append([(ci, nh, ci == mine[0], ci == mine[-1]) for ci in mine[j : j + 2]])
-        n_pairs = len(pairs)
+                for j in range(0, len(mine), 2):
+                    jobs.append([(ci, 0, HALF, ci == mine[0], ci == mine[-1]) for ci in mine[j : j + 2]])
+                for q in (2, 3):
+                    jobs.append([(ci, QUARTER * q, QUARTER, ci == mine[0], ci == mine[-1]) for ci in mine])
+        n_jobs = len(jobs)
 
-        act_sb = []
-        for a in range(3):
-            t = keep.tile([P, BT, K], BF16, name="act%d" % a)
-            nc.sync.dma_start(out=t[:], in_=acts_dram[a].rearrange("(p t) k -> p t k", t=BT))
-            act_sb.append(t)
-        raw_tiles = []
-        for ci, (gi, a, w, g) in enumerate(chunks):
-            r = rawp.tile([P, PACK, NCOL], BF16, name="raw%d" % ci, tag="raw")
-            nc.sync.dma_start(
-                out=r[:].rearrange("q j n -> q (j n)"),
-                in_=w[K_PASS * g : K_PASS * (g + 1), :].rearrange("(q j) n -> q (j n)", j=PACK),
-            )
-            raw_tiles.append(r)
+        act_sb = [keep.tile([P, BT, K], BF16, name="act%d" % a) for a in range(3)]
+        raw_tiles = [None] * len(chunks)
 
-        a_codes = []
-        a_scales = []
-        n_banks = 0
-        for a in range(3):
-            codes = keep.tile([P, 2, HALF], U32, name="acodes%d" % a, align_bytes=64)
-            scales = keep.tile([P, 2, HALF], U8, name="ascales%d" % a, align_bytes=64)
-            a_codes.append(codes)
-            a_scales.append(scales)
+        def load_act(a):
+            nc.sync.dma_start(out=act_sb[a][:], in_=acts_dram[a].rearrange("(p t) k -> p t k", t=BT))
+
+        def load_chunk(ci, parts):
+            gi, a, w, g = chunks[ci]
+            src = w[K_PASS * g : K_PASS * (g + 1), :].rearrange("(q j) n -> q j n", j=PACK)
+            width = NCOL // parts
+            tiles = []
+            for c in range(parts):
+                name = "raw%d_%d" % (ci, c)
+                pool = rawp if parts == 1 else keep
+                r = pool.tile([P, PACK, width], BF16, name=name, tag="raw" if parts == 1 else name)
+                nc.sync.dma_start(out=r[:], in_=src[:, :, width * c : width * (c + 1)])
+                tiles.append(r)
+            raw_tiles[ci] = tiles
+
+        load_chunk(0, 2)
+        load_act(0)
+        load_chunk(1, 1)
+        load_act(1)
+        load_chunk(2, 1)
+        load_act(2)
+        for ci in range(3, len(chunks)):
+            load_chunk(ci, 1)
+
+        a_codes = [keep.tile([P, 2, HALF], U32, name="acodes%d" % a, align_bytes=64) for a in range(3)]
+        a_scales = [keep.tile([P, 2, HALF], U8, name="ascales%d" % a, align_bytes=64) for a in range(3)]
+        a_grouped = {}
+        a_turned = {}
+
+        def turn_act(a):
             words = act_sb[a][:].bitcast(F32).rearrange("p t (g q u) -> p t g u q", g=2, u=2)
-            grouped = []
+            a_turned[a] = []
             for g in range(2):
-                ga = keep.tile([P, PACK * HALF], BF16, name="ga%d_%d" % (a, g), tag="ga%d" % g, align_bytes=64)
-                ga_w = ga[:].bitcast(F32).rearrange("q (t m u) -> q t m u", t=BT, u=2)
                 for tp in range(2):
-                    ps = psum.tile([P, 2, 2, P], F32, name="tr%d_%d_%d" % (a, g, tp), tag="b%d" % (n_banks % 8))
-                    n_banks += 1
+                    ps = psum.tile([P, 2, 2, P], F32, name="tr%d_%d_%d" % (a, g, tp), tag="b%d" % (4 * (a % 2) + 2 * g + tp))
                     for t2 in range(2):
                         for u in range(2):
                             nc.tensor.transpose(ps[:, t2, u, :], words[:, 2 * tp + t2, g, u, :], ident[:])
+                    a_turned[a].append(ps)
+
+        def unload_act(a):
+            ga = agrp.tile([P, 2, PACK * HALF], BF16, name="ga%d" % a, tag="ga", align_bytes=64)
+            for g in range(2):
+                ga_w = ga[:, g, :].bitcast(F32).rearrange("q (t m u) -> q t m u", t=BT, u=2)
+                for tp in range(2):
                     dst = ga_w[:, 2 * tp : 2 * tp + 2, :, :]
-                    src = ps[:].rearrange("q t u m -> q t m u")
+                    src = a_turned[a][2 * g + tp][:].rearrange("q t u m -> q t m u")
                     if tp == 0:
                         nc.vector.tensor_copy(out=dst, in_=src)
                     else:
                         nc.scalar.copy(out=dst, in_=src)
-                grouped.append(ga)
-            for g in range(2):
-                nc.vector.quantize_mx(
-                    out=codes[:, g, :].bitcast(FP8X4), scales=scales[:, g, :], in_=grouped[g][:]
-                )
+            a_grouped[a] = ga
 
-        a_part = keep.tile([P, 8, HALF], F32, name="a_part")
-        i_gate = keep.tile([P, 8, HALF], F32, name="i_gate")
+        def quantise_act(a):
+            nc.vector.quantize_mx(
+                out=a_codes[a][:].rearrange("p g m -> p (g m)").bitcast(FP8X4),
+                scales=a_scales[a][:].rearrange("p g m -> p (g m)"),
+                in_=a_grouped[a][:].rearrange("p g m -> p (g m)"),
+            )
+
+        a_part = keep.tile([P, 2, 4, 2, QUARTER], F32, name="a_part")
+        i_gate = keep.tile([P, 2, 4, 2, QUARTER], F32, name="i_gate")
+        c_in = act_sb[2][:].rearrange("p (tp t) (q n) -> p tp q t n", t=2, n=QUARTER)
+        out_q = out_v.rearrange("p (tp t) (q n) -> p tp q t n", t=2, n=QUARTER)
         grouped_w = {}
         coded_w = {}
         accs = {}
         c_dash = {}
 
+        def v_cols(s):
+            if s == 0:
+                return V_FIRST
+            if s == n_jobs - 1:
+                return V_LAST
+            return V_MID if chunks[jobs[s][0][0]][0] < 2 else V_C
+
+        def raw_columns(ci, c0, width):
+            tiles = raw_tiles[ci]
+            each = NCOL // len(tiles)
+            return tiles[c0 // each][:, :, c0 % each : c0 % each + width]
+
         def regroup(s):
-            gw = grp.tile([P, 2, HALF, PACK], BF16, name="gw%d" % s, tag="gw", align_bytes=64)
-            for j, (ci, nh, opens, closes) in enumerate(pairs[s]):
-                dst = gw[:, j, :, :].rearrange("p (c i) t -> p c t i", i=8)
-                src = raw_tiles[ci][:, :, HALF * nh : HALF * (nh + 1)].rearrange("p t (c i) -> p c t i", i=8)
-                if j == 0 or s == n_pairs - 1:
-                    nc.vector.tensor_copy(out=dst, in_=src)
-                else:
-                    nc.scalar.copy(out=dst, in_=src)
+            gw = grp.tile([P, NCOL, PACK], BF16, name="gw%d" % s, tag="gw", align_bytes=64)
+            at = 0
+            for ci, c0, width, opens, closes in jobs[s]:
+                cut = min(max(v_cols(s) - at, 0), width)
+                for lo, hi, copy in ((0, cut, nc.vector.tensor_copy), (cut, width, nc.scalar.copy)):
+                    if lo < hi:
+                        copy(
+                            out=gw[:, at + lo : at + hi, :].rearrange("p (c i) t -> p c t i", i=RUN),
+                            in_=raw_columns(ci, c0 + lo, hi - lo).rearrange("p t (c i) -> p c t i", i=RUN),
+                        )
+                at += width
             grouped_w[s] = gw
 
         def quantise(s):
-            wc = cod.tile([P, 2, HALF], U32, name="wc%d" % s, tag="wc", align_bytes=64)
-            ws = cod.tile([P, 2, HALF], U8, name="ws%d" % s, tag="ws", align_bytes=64)
+            wc = cod.tile([P, NCOL], U32, name="wc%d" % s, tag="wc", align_bytes=64)
+            ws = cod.tile([P, NCOL], U8, name="ws%d" % s, tag="ws", align_bytes=64)
             nc.vector.quantize_mx(
-                out=wc[:].rearrange("p j n -> p (j n)").bitcast(FP8X4),
-                scales=ws[:].rearrange("p j n -> p (j n)"),
-                in_=grouped_w[s][:].rearrange("p j n t -> p (j n t)"),
+                out=wc[:].bitcast(FP8X4),
+                scales=ws[:],
+                in_=grouped_w[s][:].rearrange("p n t -> p (n t)"),
             )
             coded_w[s] = (wc, ws)
 
-        def multiply(s):
+        def one_pass(s, u, t):
+            ci, c0, width, opens, closes = jobs[s][u]
+            gi, a, w, g = chunks[ci]
+            at = sum(unit[2] for unit in jobs[s][:u])
             wc, ws = coded_w[s]
-            for j, (ci, nh, opens, closes) in enumerate(pairs[s]):
-                gi, a, w, g = chunks[ci]
+            nc.tensor.matmul_mx(
+                out=accs[(gi, c0)][t][:],
+                lhsT=a_codes[a][:, g, P * t : P * (t + 1)].bitcast(FP8X4),
+                lhsT_scale=a_scales[a][:, g, P * t : P * (t + 1)],
+                rhs=wc[:, at : at + width].bitcast(FP8X4),
+                rhs_scale=ws[:, at : at + width],
+                start=opens,
+                stop=closes,
+            )
+
+        def open_banks(gi, c0, width):
+            first = 0 if c0 in (0, 3 * QUARTER) else BT
+            accs[(gi, c0)] = [
+                psum.tile([P, width], F32, name="acc%d_%d_%d" % (gi, c0, t), tag="b%d" % (first + t))
+                for t in range(BT)
+            ]
+
+        def multiply(s):
+            units = jobs[s]
+            for ci, c0, width, opens, closes in units:
                 if opens:
-                    accs[(gi, nh)] = [
-                        psum.tile([P, HALF], F32, name="acc%d_%d_%d" % (gi, nh, t), tag="b%d" % (BT * nh + t))
-                        for t in range(BT)
-                    ]
-                for t in range(BT):
-                    nc.tensor.matmul_mx(
-                        out=accs[(gi, nh)][t][:],
-                        lhsT=a_codes[a][:, g, P * t : P * (t + 1)].bitcast(FP8X4),
-                        lhsT_scale=a_scales[a][:, g, P * t : P * (t + 1)],
-                        rhs=wc[:, j, :].bitcast(FP8X4),
-                        rhs_scale=ws[:, j, :],
-                        start=opens,
-                        stop=closes,
-                    )
-            for ci, nh, opens, closes in pairs[s]:
-                gi = chunks[ci][0]
-                if closes:
+                    open_banks(chunks[ci][0], c0, width)
+            if chunks[units[0][0]][0] < 2:
+                for u in range(len(units)):
                     for t in range(BT):
-                        b = BT * nh + t
-                        acc = accs[(gi, nh)][t]
-                        if gi == 0:
-                            nc.scalar.activation(out=a_part[:, b, :], in_=acc[:], func=ACT.Sigmoid)
-                        elif gi == 1:
-                            nc.scalar.activation(out=i_gate[:, b, :], in_=acc[:], func=ACT.Sigmoid)
-                        else:
-                            if t % 2 == 0:
-                                c_dash[b] = tmp.tile([P, 2, HALF], F32, name="cd%d" % b, tag="cd")
-                            nc.scalar.activation(out=c_dash[b - t % 2][:, t % 2, :], in_=acc[:], func=ACT.Tanh)
+                        one_pass(s, u, t)
+            else:
+                for t in range(BT):
+                    for u in range(len(units)):
+                        one_pass(s, u, t)
+            for ci, c0, width, opens, closes in units:
+                gi = chunks[ci][0]
+                if not closes:
+                    continue
+                qs = slice(c0 // QUARTER, (c0 + width) // QUARTER)
+                for t in range(BT):
+                    acc = accs[(gi, c0)][t][:].rearrange("p (q n) -> p q n", n=QUARTER)
+                    if gi == 0:
+                        nc.scalar.activation(out=a_part[:, t // 2, qs, t % 2, :], in_=acc, func=ACT.Sigmoid)
+                    elif gi == 1:
+                        nc.scalar.activation(out=i_gate[:, t // 2, qs, t % 2, :], in_=acc, func=ACT.Sigmoid)
+                    else:
+                        if t % 2 == 0:
+                            c_dash[(c0, t)] = tmp.tile([P, width // QUARTER, 2, QUARTER], F32, name="cd%d_%d" % (c0, t), tag="cd")
+                        nc.scalar.activation(out=c_dash[(c0, t - t % 2)][:, :, t % 2, :], in_=acc, func=ACT.Tanh)
 
         def combine(s):
-            for ci, nh, opens, closes in pairs[s]:
+            for ci, c0, width, opens, closes in jobs[s]:
                 gi = chunks[ci][0]
                 if not closes or gi == 1:
                     continue
-                cols = slice(HALF * nh, HALF * (nh + 1))
-                for t in range(0, BT, 2):
-                    b = BT * nh + t
-                    part = a_part[:, b : b + 2, :]
+                qs = slice(c0 // QUARTER, (c0 + width) // QUARTER)
+                for tp in range(2):
+                    part = a_part[:, tp, qs, :, :]
                     if gi == 0:
-                        nc.vector.tensor_mul(out=part, in0=part, in1=act_sb[2][:, t : t + 2, cols])
+                        nc.vector.tensor_mul(out=part, in0=part, in1=c_in[:, tp, qs, :, :])
                     else:
-                        cd = c_dash[b]
-                        nc.vector.tensor_mul(out=cd[:], in0=cd[:], in1=i_gate[:, b : b + 2, :])
-                        nc.vector.tensor_add(out=part, in0=part, in1=cd[:])
-                        nc.sync.dma_start(out=out_v[:, t : t + 2, cols], in_=part)
+                        cd = c_dash[(c0, 2 * tp)][:]
+                        nc.vector.tensor_mul(out=cd, in0=cd, in1=i_gate[:, tp, qs, :, :])
+                        nc.vector.tensor_add(out=part, in0=part, in1=cd)
+                        for q in range(c0 // QUARTER, (c0 + width) // QUARTER):
+                            nc.sync.dma_start(out=out_q[:, tp, q, :, :], in_=a_part[:, tp, q, :, :])
 
-        for s in range(-LEAD, n_pairs + COMBINE_LAG + 1):
-            if 0 <= s < n_pairs:
+        regroup(0)
+        turn_act(0)
+        quantise(0)
+        unload_act(0)
+        turn_act(1)
+        regroup(1)
+        quantise_act(0)
+        quantise(1)
+        turn_act(2)
+        unload_act(1)
+        regroup(2)
+        quantise_act(1)
+        unload_act(2)
+        regroup(3)
+        quantise_act(2)
+        multiply(0)
+        for s in range(2, n_jobs + 2):
+            if s < n_jobs:
                 quantise(s)
-            if 0 <= s + LEAD < n_pairs:
+            if s + LEAD < n_jobs:
                 regroup(s + LEAD)
-            if 0 <= s - 1 < n_pairs:
+            if s - 1 < n_jobs:
                 multiply(s - 1)
-            if 0 <= s - 1 - COMBINE_LAG < n_pairs:
-                combine(s - 1 - COMBINE_LAG)
+            if 0 <= s - 2 < n_jobs:
+                combine(s - 2)

@@ -23,8 +23,10 @@ QUARTER = 256
 RAW_BUFS = 8
 LEAD = 2
 V_FIRST = 768
-V_MID = 512
+V_MID = 560
 V_LAST = 1024
+V_HEAD = 640
+ACT_V = 1
 V_C = 512
 GRP_BUFS = 3
 CODE_BUFS = 6
@@ -82,8 +84,10 @@ def tile_lstm_peephole_build_pa_kernel(
         for gi in range(3):
             mine = [ci for ci in range(len(chunks)) if chunks[ci][0] == gi]
             if gi < 2:
-                for ci in mine:
-                    jobs.append([(ci, HALF * nh, HALF, ci == mine[0], ci == mine[-1]) for nh in range(2)])
+                for ci in mine[:-2]:
+                    jobs.append([(ci, HALF * nh, HALF, ci == mine[0], False) for nh in range(2)])
+                for nh in range(2):
+                    jobs.append([(ci, HALF * nh, HALF, False, ci == mine[-1]) for ci in mine[-2:]])
             else:
                 for j in range(0, len(mine), 2):
                     jobs.append([(ci, 0, HALF, ci == mine[0], ci == mine[-1]) for ci in mine[j : j + 2]])
@@ -142,7 +146,7 @@ def tile_lstm_peephole_build_pa_kernel(
                 for tp in range(2):
                     dst = ga_w[:, 2 * tp : 2 * tp + 2, :, :]
                     src = a_turned[a][2 * g + tp][:].rearrange("q t u m -> q t m u")
-                    if tp == 0:
+                    if 2 * g + tp < ACT_V:
                         nc.vector.tensor_copy(out=dst, in_=src)
                     else:
                         nc.scalar.copy(out=dst, in_=src)
@@ -167,6 +171,8 @@ def tile_lstm_peephole_build_pa_kernel(
         def v_cols(s):
             if s == 0:
                 return V_FIRST
+            if s < 3:
+                return V_HEAD
             if s == n_jobs - 1:
                 return V_LAST
             return V_MID if chunks[jobs[s][0][0]][0] < 2 else V_C

@@ -23,11 +23,11 @@ QUARTER = 256
 RAW_BUFS = 8
 LEAD = 2
 V_FIRST = 768
-V_MID = 560
-V_LAST = 1024
-V_HEAD = 640
+V_MID = 480
+V_LAST = 768
+V_HEAD = 512
 ACT_V = 1
-V_C = 512
+V_C = 480
 GRP_BUFS = 3
 CODE_BUFS = 6
 RUN = 8
@@ -63,7 +63,7 @@ def tile_lstm_peephole_build_pa_kernel(
         grp = ctx.enter_context(tc.tile_pool(name="grp", bufs=GRP_BUFS))
         agrp = ctx.enter_context(tc.tile_pool(name="agrp", bufs=2))
         cod = ctx.enter_context(tc.tile_pool(name="cod", bufs=CODE_BUFS))
-        tmp = ctx.enter_context(tc.tile_pool(name="tmp", bufs=4))
+        tmp = ctx.enter_context(tc.tile_pool(name="tmp", bufs=6))
         psum = ctx.enter_context(tc.psum_pool(name="psum", bufs=1))
         ctx.enter_context(tc.manual_schedule())
 
@@ -95,11 +95,14 @@ def tile_lstm_peephole_build_pa_kernel(
                     jobs.append([(ci, QUARTER * q, QUARTER, ci == mine[0], ci == mine[-1]) for ci in mine])
         n_jobs = len(jobs)
 
-        act_sb = [keep.tile([P, BT, K], BF16, name="act%d" % a) for a in range(3)]
+        act_sb = [None] * 3
         raw_tiles = [None] * len(chunks)
 
         def load_act(a):
-            nc.sync.dma_start(out=act_sb[a][:], in_=acts_dram[a].rearrange("(p t) k -> p t k", t=BT))
+            pool = keep if a == 2 else rawp
+            t = pool.tile([P, BT, K], BF16, name="act%d" % a, tag="act" if a == 2 else "raw")
+            nc.sync.dma_start(out=t[:], in_=acts_dram[a].rearrange("(p t) k -> p t k", t=BT))
+            act_sb[a] = t
 
         def load_chunk(ci, parts):
             gi, a, w, g = chunks[ci]
@@ -159,10 +162,8 @@ def tile_lstm_peephole_build_pa_kernel(
                 in_=a_grouped[a][:].rearrange("p g m -> p (g m)"),
             )
 
-        a_part = keep.tile([P, 2, 4, 2, QUARTER], F32, name="a_part")
-        i_gate = keep.tile([P, 2, 4, 2, QUARTER], F32, name="i_gate")
-        c_in = act_sb[2][:].rearrange("p (tp t) (q n) -> p tp q t n", t=2, n=QUARTER)
-        out_q = out_v.rearrange("p (tp t) (q n) -> p tp q t n", t=2, n=QUARTER)
+        f_part = [keep.tile([P, BT, HALF], F32, name="f_part%d" % nh) for nh in range(2)]
+        i_gate = [keep.tile([P, BT, HALF], F32, name="i_gate%d" % nh) for nh in range(2)]
         grouped_w = {}
         coded_w = {}
         accs = {}
@@ -245,34 +246,38 @@ def tile_lstm_peephole_build_pa_kernel(
                 gi = chunks[ci][0]
                 if not closes:
                     continue
-                qs = slice(c0 // QUARTER, (c0 + width) // QUARTER)
                 for t in range(BT):
-                    acc = accs[(gi, c0)][t][:].rearrange("p (q n) -> p q n", n=QUARTER)
+                    acc = accs[(gi, c0)][t][:]
                     if gi == 0:
-                        nc.scalar.activation(out=a_part[:, t // 2, qs, t % 2, :], in_=acc, func=ACT.Sigmoid)
+                        nc.scalar.activation(out=f_part[c0 // HALF][:, t, :], in_=acc, func=ACT.Sigmoid)
                     elif gi == 1:
-                        nc.scalar.activation(out=i_gate[:, t // 2, qs, t % 2, :], in_=acc, func=ACT.Sigmoid)
+                        nc.scalar.activation(out=i_gate[c0 // HALF][:, t, :], in_=acc, func=ACT.Sigmoid)
                     else:
                         if t % 2 == 0:
-                            c_dash[(c0, t)] = tmp.tile([P, width // QUARTER, 2, QUARTER], F32, name="cd%d_%d" % (c0, t), tag="cd")
-                        nc.scalar.activation(out=c_dash[(c0, t - t % 2)][:, :, t % 2, :], in_=acc, func=ACT.Tanh)
+                            c_dash[(c0, t)] = tmp.tile([P, 2, width], F32, name="cd%d_%d" % (c0, t), tag="cd")
+                        nc.scalar.activation(out=c_dash[(c0, t - t % 2)][:, t % 2, :], in_=acc, func=ACT.Tanh)
 
         def combine(s):
             for ci, c0, width, opens, closes in jobs[s]:
                 gi = chunks[ci][0]
                 if not closes or gi == 1:
                     continue
-                qs = slice(c0 // QUARTER, (c0 + width) // QUARTER)
-                for tp in range(2):
-                    part = a_part[:, tp, qs, :, :]
-                    if gi == 0:
-                        nc.vector.tensor_mul(out=part, in0=part, in1=c_in[:, tp, qs, :, :])
-                    else:
-                        cd = c_dash[(c0, 2 * tp)][:]
-                        nc.vector.tensor_mul(out=cd, in0=cd, in1=i_gate[:, tp, qs, :, :])
-                        nc.vector.tensor_add(out=part, in0=part, in1=cd)
-                        for q in range(c0 // QUARTER, (c0 + width) // QUARTER):
-                            nc.sync.dma_start(out=out_q[:, tp, q, :, :], in_=a_part[:, tp, q, :, :])
+                cols = slice(c0, c0 + width)
+                at = slice(c0 % HALF, c0 % HALF + width)
+                f_half = f_part[c0 // HALF]
+                i_half = i_gate[c0 // HALF]
+                if gi == 0:
+                    for t in range(0, BT, 2):
+                        part = f_half[:, t : t + 2, :]
+                        nc.vector.tensor_mul(out=part, in0=part, in1=act_sb[2][:, t : t + 2, cols])
+                    continue
+                for t in range(0, BT, 2):
+                    cd = c_dash[(c0, t)][:]
+                    nc.vector.tensor_mul(out=cd, in0=cd, in1=i_half[:, t : t + 2, at])
+                for t in range(0, BT, 2):
+                    cd = c_dash[(c0, t)][:]
+                    nc.vector.tensor_add(out=cd, in0=cd, in1=f_half[:, t : t + 2, at])
+                    nc.sync.dma_start(out=out_v[:, t : t + 2, cols], in_=cd)
 
         regroup(0)
         turn_act(0)

@@ -23,11 +23,11 @@ QUARTER = 256
 RAW_BUFS = 8
 LEAD = 2
 V_FIRST = 768
-V_MID = 480
-V_LAST = 768
+V_MID = 544
+V_LAST = 1024
 V_HEAD = 512
 ACT_V = 1
-V_C = 480
+V_C = 512
 GRP_BUFS = 3
 CODE_BUFS = 6
 RUN = 8
@@ -286,20 +286,21 @@ def tile_lstm_peephole_build_pa_kernel(
         turn_act(1)
         regroup(1)
         quantise_act(0)
-        quantise(1)
         turn_act(2)
         unload_act(1)
         regroup(2)
+        quantise(1)
         quantise_act(1)
         unload_act(2)
         regroup(3)
-        quantise_act(2)
         multiply(0)
         for s in range(2, n_jobs + 2):
             if s < n_jobs:
                 quantise(s)
             if s + LEAD < n_jobs:
                 regroup(s + LEAD)
+            if s == 2:
+                quantise_act(2)
             if s - 1 < n_jobs:
                 multiply(s - 1)
             if 0 <= s - 2 < n_jobs:

from contextlib import ExitStack

import concourse.mybir as mybir
from concourse.masks import make_identity

FLOPS = 2 * 512 * 1024 * 1024 * 8

F32 = mybir.dt.float32
BF16 = mybir.dt.bfloat16
U32 = mybir.dt.uint32
U8 = mybir.dt.uint8
FP8X4 = mybir.dt.float8_e4m3fn_x4
ACT = mybir.ActivationFunctionType

P = 128
PACK = 4
BT = 4
K = 1024
K_PASS = 512
NCOL = 1024
HALF = 512
QUARTER = 256
RAW_BUFS = 8
LEAD = 2
V_FIRST = 768
V_MID = 544
V_LAST = 1024
V_HEAD = 512
ACT_V = 1
V_C = 512
GRP_BUFS = 3
CODE_BUFS = 6
RUN = 8


def tile_lstm_peephole_build_pa_kernel(
    tc,
    input_data,
    previous_hidden_state,
    previous_c_state,
    w_forget,
    w_input,
    w_c_dash,
    w_forget_c,
    w_input_c,
    w_ip_f,
    w_ip_i,
    w_ip_c_dash,
    out,
):
    nc = tc.nc
    acts_dram = [input_data, previous_hidden_state, previous_c_state]
    gates = [
        [(0, w_ip_f), (1, w_forget), (2, w_forget_c)],
        [(0, w_ip_i), (1, w_input), (2, w_input_c)],
        [(0, w_ip_c_dash), (1, w_c_dash)],
    ]
    out_v = out.rearrange("(p t) n -> p t n", t=BT)

    with ExitStack() as ctx:
        keep = ctx.enter_context(tc.tile_pool(name="keep", bufs=1))
        rawp = ctx.enter_context(tc.tile_pool(name="rawp", bufs=RAW_BUFS))
        grp = ctx.enter_context(tc.tile_pool(name="grp", bufs=GRP_BUFS))
        agrp = ctx.enter_context(tc.tile_pool(name="agrp", bufs=2))
        cod = ctx.enter_context(tc.tile_pool(name="cod", bufs=CODE_BUFS))
        tmp = ctx.enter_context(tc.tile_pool(name="tmp", bufs=6))
        psum = ctx.enter_context(tc.psum_pool(name="psum", bufs=1))
        ctx.enter_context(tc.manual_schedule())

        ident = keep.tile([P, P], F32, name="ident")
        make_identity(nc, ident[:])
        warm_in = keep.tile([P, 1], F32, name="warm_in")
        warm_out = keep.tile([P, 1], F32, name="warm_out")
        nc.vector.memset(warm_in[:], 0.0)
        nc.scalar.activation(out=warm_out[:], in_=warm_in[:], func=ACT.Sigmoid)

        chunks = []
        for gi, products in enumerate(gates):
            for a, w in products:
                for g in range(2):
                    chunks.append((gi, a, w, g))

        jobs = []
        for gi in range(3):
            mine = [ci for ci in range(len(chunks)) if chunks[ci][0] == gi]
            if gi < 2:
                for ci in mine[:-2]:
                    jobs.append([(ci, HALF * nh, HALF, ci == mine[0], False) for nh in range(2)])
                for nh in range(2):
                    jobs.append([(ci, HALF * nh, HALF, False, ci == mine[-1]) for ci in mine[-2:]])
            else:
                for j in range(0, len(mine), 2):
                    jobs.append([(ci, 0, HALF, ci == mine[0], ci == mine[-1]) for ci in mine[j : j + 2]])
                for q in (2, 3):
                    jobs.append([(ci, QUARTER * q, QUARTER, ci == mine[0], ci == mine[-1]) for ci in mine])
        n_jobs = len(jobs)

        act_sb = [None] * 3
        raw_tiles = [None] * len(chunks)

        def load_act(a):
            pool = keep if a == 2 else rawp
            t = pool.tile([P, BT, K], BF16, name="act%d" % a, tag="act" if a == 2 else "raw")
            nc.sync.dma_start(out=t[:], in_=acts_dram[a].rearrange("(p t) k -> p t k", t=BT))
            act_sb[a] = t

        def load_chunk(ci, parts):
            gi, a, w, g = chunks[ci]
            src = w[K_PASS * g : K_PASS * (g + 1), :].rearrange("(q j) n -> q j n", j=PACK)
            width = NCOL // parts
            tiles = []
            for c in range(parts):
                name = "raw%d_%d" % (ci, c)
                pool = rawp if parts == 1 else keep
                r = pool.tile([P, PACK, width], BF16, name=name, tag="raw" if parts == 1 else name)
                nc.sync.dma_start(out=r[:], in_=src[:, :, width * c : width * (c + 1)])
                tiles.append(r)
            raw_tiles[ci] = tiles

        load_chunk(0, 2)
        load_act(0)
        load_chunk(1, 1)
        load_act(1)
        load_chunk(2, 1)
        load_act(2)
        for ci in range(3, len(chunks)):
            load_chunk(ci, 1)

        a_codes = [keep.tile([P, 2, HALF], U32, name="acodes%d" % a, align_bytes=64) for a in range(3)]
        a_scales = [keep.tile([P, 2, HALF], U8, name="ascales%d" % a, align_bytes=64) for a in range(3)]
        a_grouped = {}
        a_turned = {}

        def turn_act(a):
            words = act_sb[a][:].bitcast(F32).rearrange("p t (g q u) -> p t g u q", g=2, u=2)
            a_turned[a] = []
            for g in range(2):
                for tp in range(2):
                    ps = psum.tile([P, 2, 2, P], F32, name="tr%d_%d_%d" % (a, g, tp), tag="b%d" % (4 * (a % 2) + 2 * g + tp))
                    for t2 in range(2):
                        for u in range(2):
                            nc.tensor.transpose(ps[:, t2, u, :], words[:, 2 * tp + t2, g, u, :], ident[:])
                    a_turned[a].append(ps)

        def unload_act(a):
            ga = agrp.tile([P, 2, PACK * HALF], BF16, name="ga%d" % a, tag="ga", align_bytes=64)
            for g in range(2):
                ga_w = ga[:, g, :].bitcast(F32).rearrange("q (t m u) -> q t m u", t=BT, u=2)
                for tp in range(2):
                    dst = ga_w[:, 2 * tp : 2 * tp + 2, :, :]
                    src = a_turned[a][2 * g + tp][:].rearrange("q t u m -> q t m u")
                    if 2 * g + tp < ACT_V:
                        nc.vector.tensor_copy(out=dst, in_=src)
                    else:
                        nc.scalar.copy(out=dst, in_=src)
            a_grouped[a] = ga

        def quantise_act(a):
            nc.vector.quantize_mx(
                out=a_codes[a][:].rearrange("p g m -> p (g m)").bitcast(FP8X4),
                scales=a_scales[a][:].rearrange("p g m -> p (g m)"),
                in_=a_grouped[a][:].rearrange("p g m -> p (g m)"),
            )

        f_part = [keep.tile([P, BT, HALF], F32, name="f_part%d" % nh) for nh in range(2)]
        i_gate = [keep.tile([P, BT, HALF], F32, name="i_gate%d" % nh) for nh in range(2)]
        grouped_w = {}
        coded_w = {}
        accs = {}
        c_dash = {}

        def v_cols(s):
            if s == 0:
                return V_FIRST
            if s < 3:
                return V_HEAD
            if s == n_jobs - 1:
                return V_LAST
            return V_MID if chunks[jobs[s][0][0]][0] < 2 else V_C

        def raw_columns(ci, c0, width):
            tiles = raw_tiles[ci]
            each = NCOL // len(tiles)
            return tiles[c0 // each][:, :, c0 % each : c0 % each + width]

        def regroup(s):
            gw = grp.tile([P, NCOL, PACK], BF16, name="gw%d" % s, tag="gw", align_bytes=64)
            at = 0
            for ci, c0, width, opens, closes in jobs[s]:
                cut = min(max(v_cols(s) - at, 0), width)
                for lo, hi, copy in ((0, cut, nc.vector.tensor_copy), (cut, width, nc.scalar.copy)):
                    if lo < hi:
                        copy(
                            out=gw[:, at + lo : at + hi, :].rearrange("p (c i) t -> p c t i", i=RUN),
                            in_=raw_columns(ci, c0 + lo, hi - lo).rearrange("p t (c i) -> p c t i", i=RUN),
                        )
                at += width
            grouped_w[s] = gw

        def quantise(s):
            wc = cod.tile([P, NCOL], U32, name="wc%d" % s, tag="wc", align_bytes=64)
            ws = cod.tile([P, NCOL], U8, name="ws%d" % s, tag="ws", align_bytes=64)
            nc.vector.quantize_mx(
                out=wc[:].bitcast(FP8X4),
                scales=ws[:],
                in_=grouped_w[s][:].rearrange("p n t -> p (n t)"),
            )
            coded_w[s] = (wc, ws)

        def one_pass(s, u, t):
            ci, c0, width, opens, closes = jobs[s][u]
            gi, a, w, g = chunks[ci]
            at = sum(unit[2] for unit in jobs[s][:u])
            wc, ws = coded_w[s]
            nc.tensor.matmul_mx(
                out=accs[(gi, c0)][t][:],
                lhsT=a_codes[a][:, g, P * t : P * (t + 1)].bitcast(FP8X4),
                lhsT_scale=a_scales[a][:, g, P * t : P * (t + 1)],
                rhs=wc[:, at : at + width].bitcast(FP8X4),
                rhs_scale=ws[:, at : at + width],
                start=opens,
                stop=closes,
            )

        def open_banks(gi, c0, width):
            first = 0 if c0 in (0, 3 * QUARTER) else BT
            accs[(gi, c0)] = [
                psum.tile([P, width], F32, name="acc%d_%d_%d" % (gi, c0, t), tag="b%d" % (first + t))
                for t in range(BT)
            ]

        def multiply(s):
            units = jobs[s]
            for ci, c0, width, opens, closes in units:
                if opens:
                    open_banks(chunks[ci][0], c0, width)
            if chunks[units[0][0]][0] < 2:
                for u in range(len(units)):
                    for t in range(BT):
                        one_pass(s, u, t)
            else:
                for t in range(BT):
                    for u in range(len(units)):
                        one_pass(s, u, t)
            for ci, c0, width, opens, closes in units:
                gi = chunks[ci][0]
                if not closes:
                    continue
                for t in range(BT):
                    acc = accs[(gi, c0)][t][:]
                    if gi == 0:
                        nc.scalar.activation(out=f_part[c0 // HALF][:, t, :], in_=acc, func=ACT.Sigmoid)
                    elif gi == 1:
                        nc.scalar.activation(out=i_gate[c0 // HALF][:, t, :], in_=acc, func=ACT.Sigmoid)
                    else:
                        if t % 2 == 0:
                            c_dash[(c0, t)] = tmp.tile([P, 2, width], F32, name="cd%d_%d" % (c0, t), tag="cd")
                        nc.scalar.activation(out=c_dash[(c0, t - t % 2)][:, t % 2, :], in_=acc, func=ACT.Tanh)

        def combine(s):
            for ci, c0, width, opens, closes in jobs[s]:
                gi = chunks[ci][0]
                if not closes or gi == 1:
                    continue
                cols = slice(c0, c0 + width)
                at = slice(c0 % HALF, c0 % HALF + width)
                f_half = f_part[c0 // HALF]
                i_half = i_gate[c0 // HALF]
                if gi == 0:
                    for t in range(0, BT, 2):
                        part = f_half[:, t : t + 2, :]
                        nc.vector.tensor_mul(out=part, in0=part, in1=act_sb[2][:, t : t + 2, cols])
                    continue
                for t in range(0, BT, 2):
                    cd = c_dash[(c0, t)][:]
                    nc.vector.tensor_mul(out=cd, in0=cd, in1=i_half[:, t : t + 2, at])
                for t in range(0, BT, 2):
                    cd = c_dash[(c0, t)][:]
                    nc.vector.tensor_add(out=cd, in0=cd, in1=f_half[:, t : t + 2, at])
                    nc.sync.dma_start(out=out_v[:, t : t + 2, cols], in_=cd)

        regroup(0)
        turn_act(0)
        quantise(0)
        unload_act(0)
        turn_act(1)
        regroup(1)
        quantise_act(0)
        turn_act(2)
        unload_act(1)
        regroup(2)
        quantise(1)
        quantise_act(1)
        unload_act(2)
        regroup(3)
        multiply(0)
        for s in range(2, n_jobs + 2):
            if s < n_jobs:
                quantise(s)
            if s + LEAD < n_jobs:
                regroup(s + LEAD)
            if s == 2:
                quantise_act(2)
            if s - 1 < n_jobs:
                multiply(s - 1)
            if 0 <= s - 2 < n_jobs:
                combine(s - 2)
